import numpy as np
import ml_dtypes

BF16 = ml_dtypes.bfloat16


def bf(x):
    return np.asarray(x, np.float32).astype(BF16)


def f32(x):
    return np.asarray(x, np.float32)


def f64(x):
    return np.asarray(x).astype(np.float64)


def striped(idx):
    return np.tile(idx.reshape(-1, 16).T, (8, 1))


C, F, S, N, Q = 128, 256, 256, 128, 2
XAV = np.sqrt(6.0 / (F + C))


def sigmoid(v):
    return 1.0 / (1.0 + np.exp(-v))


def setup_inputs():
    return {
        "base": f32(np.random.standard_normal((C, S))),
        "conv": bf(np.random.standard_normal((F, N))),
        "x": bf(np.random.standard_normal((C, N))),
        "h": f32(np.random.standard_normal((C, N))),
        "q": f32(np.random.standard_normal((Q, N))),
        "w_ru": bf(np.random.uniform(-XAV, XAV, (F, Q * F))),
        "b_ru": f32(0.5 * np.random.standard_normal((Q * F, 1))),
        "w_c": bf(np.random.uniform(-XAV, XAV, (C, Q * C))),
        "b_c": f32(0.5 * np.random.standard_normal((Q * C, 1))),
        "offs": striped(np.random.permutation(S)[:N]),
    }


def reference(base, conv, x, h, q, w_ru, b_ru, w_c, b_c, offs):
    idx = offs[:16].T.reshape(-1)
    qq = f64(q)[:, None, :]
    pre = ((f64(w_ru).T @ f64(conv) + f64(b_ru)).reshape(Q, F, N) * qq).sum(axis=0)
    r = sigmoid(pre[:C])
    u = sigmoid(pre[C:])
    cand = np.tanh(((f64(w_c).T @ f64(x) + f64(b_c)).reshape(Q, C, N) * qq).sum(axis=0))
    out = f64(base).copy()
    out[:, idx] = (1.0 - u) * r * f64(h) + u * cand
    return out

@@ -1,0 +1,121 @@
+import concourse.mybir as mybir
+
+F32 = mybir.dt.float32
+BF16 = mybir.dt.bfloat16
+U16 = mybir.dt.uint16
+ALU = mybir.AluOpType
+FUNC = mybir.ActivationFunctionType
+
+P = 128
+N = 128
+S = 256
+D = 2
+KB = 2
+WARM_UP_PRODUCTS = 4
+
+FLOPS = 2 * (KB * P) * (D * 2 * P) * N + 2 * P * (D * P) * N
+
+
+def tile_agcrncellwithmlp_kernel(tc, base, conv, x, h, q, w_ru, b_ru, w_c, b_c, offs, out):
+    nc = tc.nc
+    with tc.tile_pool(name="held", bufs=1) as held, tc.psum_pool(name="psum", bufs=1) as psum:
+        offsets = held.tile([P, N // 16], U16, name="offsets")
+        w_ru_sb = [held.tile([P, KB, 2 * P], BF16, name="w_ru_sb%d" % d) for d in range(D)]
+        conv_sb = held.tile([P, KB, N], BF16, name="conv_sb")
+        q_row = held.tile([1, D * N], F32, name="q_row")
+        b_rows = held.tile([D * 3, P], F32, name="b_rows")
+        w_c_sb = held.tile([P, D * P], BF16, name="w_c_sb")
+        x_sb = held.tile([P, N], BF16, name="x_sb")
+        h_sb = held.tile([P, N], F32, name="h_sb")
+        store = held.tile([P, S], F32, name="store")
+
+        w_ru_blocks = w_ru.rearrange("(p kb) e -> p kb e", kb=KB)
+        nc.sync.dma_start(q_row[:], q.rearrange("d j -> (d j)").unsqueeze(0))
+        nc.scalar.dma_start(b_rows[0 : D * 2, :], b_ru.rearrange("(c p) o -> c (p o)", p=P))
+        nc.sync.dma_start(w_ru_sb[0][:], w_ru_blocks[:, :, 0 : 2 * P])
+        nc.scalar.dma_start(b_rows[D * 2 : D * 3, :], b_c.rearrange("(c p) o -> c (p o)", p=P))
+        nc.sync.dma_start(w_ru_sb[1][:], w_ru_blocks[:, :, 2 * P : 4 * P])
+        nc.scalar.dma_start(conv_sb[:], conv.rearrange("(p kb) j -> p kb j", kb=KB))
+        nc.sync.dma_start(w_c_sb[:], w_c)
+        nc.sync.dma_start(x_sb[:], x)
+        nc.sync.dma_start(h_sb[:], h)
+        nc.sync.dma_start(store[:], base)
+        nc.sync.dma_start(offsets[:], offs)
+
+        zeros = held.tile([P, D * N], BF16, name="zeros")
+        nc.vector.memset(zeros[:], 0.0)
+        q_bank = psum.tile([P, D * N], F32, name="q_bank")
+        for i in range(WARM_UP_PRODUCTS):
+            nc.tensor.matmul(q_bank[:], zeros[:, 0:P], zeros[:], start=True, stop=True)
+
+        ones_row = held.tile([1, P], F32, name="ones_row")
+        nc.vector.memset(ones_row[:], 1.0)
+        identity = held.tile([D * 3, D * 3], F32, name="identity")
+        nc.vector.memset(identity[:], 0.0)
+        for k in range(D * 3):
+            nc.vector.memset(identity[0 : k + 1, k : k + 1], 1.0)
+        for k in range(1, D * 3):
+            nc.vector.memset(identity[0:k, k : k + 1], 0.0)
+
+        nc.tensor.matmul(q_bank[:], ones_row[:], q_row[:], start=True, stop=True)
+        q_sb = held.tile([P, D * N], F32, name="q_sb")
+        nc.vector.tensor_copy(q_sb[:], q_bank[:])
+
+        bias_bank = psum.tile([P, D * 3], F32, name="bias_bank")
+        nc.tensor.matmul(bias_bank[:], b_rows[:], identity[:], start=True, stop=True)
+        biases = held.tile([P, D * 3], F32, name="biases")
+        nc.vector.tensor_copy(biases[:], bias_bank[:])
+
+        scaled = {}
+        for gate in ("r", "u", "c"):
+            scaled[gate] = held.tile([P, D, N], F32, name="scaled_" + gate)
+
+        def product_and_scaling(gate, d, pairs, bias):
+            bank = psum.tile([P, N], F32, name="bank_%s%d" % (gate, d))
+            for k, (weights, moving) in enumerate(pairs):
+                nc.tensor.matmul(bank[:], weights, moving, start=(k == 0), stop=(k == len(pairs) - 1))
+            nc.vector.scalar_tensor_tensor(
+                scaled[gate][:, d, :], bank[:], bias, q_sb[:, d * N : (d + 1) * N], ALU.add, ALU.mult
+            )
+
+        def mixed(gate):
+            pre = held.tile([P, N], F32, name="pre_" + gate)
+            nc.vector.tensor_tensor(pre[:], scaled[gate][:, 0, :], scaled[gate][:, 1, :], ALU.add)
+            return pre
+
+        for d in range(D):
+            for g, gate in enumerate(("r", "u")):
+                product_and_scaling(
+                    gate,
+                    d,
+                    [(w_ru_sb[d][:, kb, g * P : (g + 1) * P], conv_sb[:, kb, :]) for kb in range(KB)],
+                    biases[:, 2 * d + g : 2 * d + g + 1],
+                )
+
+        pre_r = mixed("r")
+        r = held.tile([P, N], F32, name="r")
+        nc.scalar.activation(r[:], pre_r[:], FUNC.Sigmoid)
+
+        pre_u = mixed("u")
+        one_minus_u = held.tile([P, N], F32, name="one_minus_u")
+        nc.scalar.activation(one_minus_u[:], pre_u[:], FUNC.Sigmoid, scale=-1.0)
+        u = held.tile([P, N], F32, name="u")
+        nc.scalar.activation(u[:], pre_u[:], FUNC.Sigmoid)
+
+        for d in range(D):
+            product_and_scaling(
+                "c", d, [(w_c_sb[:, d * P : (d + 1) * P], x_sb[:])], biases[:, 2 * D + d : 2 * D + d + 1]
+            )
+        pre_c = mixed("c")
+        cand = held.tile([P, N], F32, name="cand")
+        nc.scalar.activation(cand[:], pre_c[:], FUNC.Tanh)
+
+        r_h = held.tile([P, N], F32, name="r_h")
+        nc.vector.tensor_tensor(r_h[:], r[:], h_sb[:], ALU.mult)
+        kept = held.tile([P, N], F32, name="kept")
+        nc.vector.tensor_tensor(kept[:], one_minus_u[:], r_h[:], ALU.mult)
+        fresh = held.tile([P, N], F32, name="fresh")
+        nc.vector.tensor_tensor(fresh[:], u[:], cand[:], ALU.mult)
+        nc.vector.tensor_tensor(store[:].indirect(offsets[:]), kept[:], fresh[:], ALU.add)
+
+        nc.sync.dma_start(out, store[:])

@@ -23,7 +23,8 @@ def tile_agcrncellwithmlp_kernel(tc, base, conv, x, h, q, w_ru, b_ru, w_c, b_c, 
         w_ru_sb = [held.tile([P, KB, 2 * P], BF16, name="w_ru_sb%d" % d) for d in range(D)]
         conv_sb = held.tile([P, KB, N], BF16, name="conv_sb")
         q_row = held.tile([1, D * N], F32, name="q_row")
-        b_rows = held.tile([D * 3, P], F32, name="b_rows")
+        b_ru_rows = held.tile([D * 2, P], F32, name="b_ru_rows")
+        b_c_rows = held.tile([D, P], F32, name="b_c_rows")
         w_c_sb = held.tile([P, D * P], BF16, name="w_c_sb")
         x_sb = held.tile([P, N], BF16, name="x_sb")
         h_sb = held.tile([P, N], F32, name="h_sb")
@@ -31,11 +32,11 @@ def tile_agcrncellwithmlp_kernel(tc, base, conv, x, h, q, w_ru, b_ru, w_c, b_c, 
 
         w_ru_blocks = w_ru.rearrange("(p kb) e -> p kb e", kb=KB)
         nc.sync.dma_start(q_row[:], q.rearrange("d j -> (d j)").unsqueeze(0))
-        nc.scalar.dma_start(b_rows[0 : D * 2, :], b_ru.rearrange("(c p) o -> c (p o)", p=P))
-        nc.sync.dma_start(w_ru_sb[0][:], w_ru_blocks[:, :, 0 : 2 * P])
-        nc.scalar.dma_start(b_rows[D * 2 : D * 3, :], b_c.rearrange("(c p) o -> c (p o)", p=P))
-        nc.sync.dma_start(w_ru_sb[1][:], w_ru_blocks[:, :, 2 * P : 4 * P])
         nc.scalar.dma_start(conv_sb[:], conv.rearrange("(p kb) j -> p kb j", kb=KB))
+        nc.sync.dma_start(b_ru_rows[:], b_ru.rearrange("(c p) o -> c (p o)", p=P))
+        nc.scalar.dma_start(b_c_rows[:], b_c.rearrange("(c p) o -> c (p o)", p=P))
+        nc.sync.dma_start(w_ru_sb[0][:], w_ru_blocks[:, :, 0 : 2 * P])
+        nc.sync.dma_start(w_ru_sb[1][:], w_ru_blocks[:, :, 2 * P : 4 * P])
         nc.sync.dma_start(w_c_sb[:], w_c)
         nc.sync.dma_start(x_sb[:], x)
         nc.sync.dma_start(h_sb[:], h)
@@ -50,11 +51,11 @@ def tile_agcrncellwithmlp_kernel(tc, base, conv, x, h, q, w_ru, b_ru, w_c, b_c, 
 
         ones_row = held.tile([1, P], F32, name="ones_row")
         nc.vector.memset(ones_row[:], 1.0)
-        identity = held.tile([D * 3, D * 3], F32, name="identity")
+        identity = held.tile([D * 2, D * 2], F32, name="identity")
         nc.vector.memset(identity[:], 0.0)
-        for k in range(D * 3):
+        for k in range(D * 2):
             nc.vector.memset(identity[0 : k + 1, k : k + 1], 1.0)
-        for k in range(1, D * 3):
+        for k in range(1, D * 2):
             nc.vector.memset(identity[0:k, k : k + 1], 0.0)
 
         nc.tensor.matmul(q_bank[:], ones_row[:], q_row[:], start=True, stop=True)
@@ -62,9 +63,9 @@ def tile_agcrncellwithmlp_kernel(tc, base, conv, x, h, q, w_ru, b_ru, w_c, b_c, 
         nc.vector.tensor_copy(q_sb[:], q_bank[:])
 
         bias_bank = psum.tile([P, D * 3], F32, name="bias_bank")
-        nc.tensor.matmul(bias_bank[:], b_rows[:], identity[:], start=True, stop=True)
-        biases = held.tile([P, D * 3], F32, name="biases")
-        nc.vector.tensor_copy(biases[:], bias_bank[:])
+        nc.tensor.matmul(bias_bank[:, 0 : D * 2], b_ru_rows[:], identity[:], start=True, stop=True)
+        ru_biases = held.tile([P, D * 2], F32, name="ru_biases")
+        nc.vector.tensor_copy(ru_biases[:], bias_bank[:, 0 : D * 2])
 
         scaled = {}
         for gate in ("r", "u", "c"):
@@ -89,8 +90,12 @@ def tile_agcrncellwithmlp_kernel(tc, base, conv, x, h, q, w_ru, b_ru, w_c, b_c, 
                     gate,
                     d,
                     [(w_ru_sb[d][:, kb, g * P : (g + 1) * P], conv_sb[:, kb, :]) for kb in range(KB)],
-                    biases[:, 2 * d + g : 2 * d + g + 1],
+                    ru_biases[:, 2 * d + g : 2 * d + g + 1],
                 )
+
+        nc.tensor.matmul(bias_bank[:, D * 2 : D * 3], b_c_rows[:], identity[0:D, 0:D], start=True, stop=True)
+        c_biases = held.tile([P, D], F32, name="c_biases")
+        nc.scalar.copy(c_biases[:], bias_bank[:, D * 2 : D * 3])
 
         pre_r = mixed("r")
         r = held.tile([P, N], F32, name="r")
@@ -104,7 +109,7 @@ def tile_agcrncellwithmlp_kernel(tc, base, conv, x, h, q, w_ru, b_ru, w_c, b_c, 
 
         for d in range(D):
             product_and_scaling(
-                "c", d, [(w_c_sb[:, d * P : (d + 1) * P], x_sb[:])], biases[:, 2 * D + d : 2 * D + d + 1]
+                "c", d, [(w_c_sb[:, d * P : (d + 1) * P], x_sb[:])], c_biases[:, d : d + 1]
             )
         pre_c = mixed("c")
         cand = held.tile([P, N], F32, name="cand")

@@ -33,7 +33,7 @@ def tile_agcrncellwithmlp_kernel(tc, base, conv, x, h, q, w_ru, b_ru, w_c, b_c, 
         w_ru_blocks = w_ru.rearrange("(p kb) e -> p kb e", kb=KB)
         nc.sync.dma_start(q_row[:], q.rearrange("d j -> (d j)").unsqueeze(0))
         nc.scalar.dma_start(conv_sb[:], conv.rearrange("(p kb) j -> p kb j", kb=KB))
-        nc.sync.dma_start(b_ru_rows[:], b_ru.rearrange("(c p) o -> c (p o)", p=P))
+        nc.scalar.dma_start(b_ru_rows[:], b_ru.rearrange("(c p) o -> c (p o)", p=P))
         nc.scalar.dma_start(b_c_rows[:], b_c.rearrange("(c p) o -> c (p o)", p=P))
         nc.sync.dma_start(w_ru_sb[0][:], w_ru_blocks[:, :, 0 : 2 * P])
         nc.sync.dma_start(w_ru_sb[1][:], w_ru_blocks[:, :, 2 * P : 4 * P])
@@ -94,8 +94,6 @@ def tile_agcrncellwithmlp_kernel(tc, base, conv, x, h, q, w_ru, b_ru, w_c, b_c, 
                 )
 
         nc.tensor.matmul(bias_bank[:, D * 2 : D * 3], b_c_rows[:], identity[0:D, 0:D], start=True, stop=True)
-        c_biases = held.tile([P, D], F32, name="c_biases")
-        nc.scalar.copy(c_biases[:], bias_bank[:, D * 2 : D * 3])
 
         pre_r = mixed("r")
         r = held.tile([P, N], F32, name="r")
@@ -109,7 +107,7 @@ def tile_agcrncellwithmlp_kernel(tc, base, conv, x, h, q, w_ru, b_ru, w_c, b_c, 
 
         for d in range(D):
             product_and_scaling(
-                "c", d, [(w_c_sb[:, d * P : (d + 1) * P], x_sb[:])], c_biases[:, d : d + 1]
+                "c", d, [(w_c_sb[:, d * P : (d + 1) * P], x_sb[:])], bias_bank[:, D * 2 + d : D * 2 + d + 1]
             )
         pre_c = mixed("c")
         cand = held.tile([P, N], F32, name="cand")

import concourse.mybir as mybir

F32 = mybir.dt.float32
BF16 = mybir.dt.bfloat16
U16 = mybir.dt.uint16
ALU = mybir.AluOpType
FUNC = mybir.ActivationFunctionType

P = 128
N = 128
S = 256
D = 2
KB = 2
WARM_UP_PRODUCTS = 4

FLOPS = 2 * (KB * P) * (D * 2 * P) * N + 2 * P * (D * P) * N


def tile_agcrncellwithmlp_kernel(tc, base, conv, x, h, q, w_ru, b_ru, w_c, b_c, offs, out):
    nc = tc.nc
    with tc.tile_pool(name="held", bufs=1) as held, tc.psum_pool(name="psum", bufs=1) as psum:
        offsets = held.tile([P, N // 16], U16, name="offsets")
        w_ru_sb = [held.tile([P, KB, 2 * P], BF16, name="w_ru_sb%d" % d) for d in range(D)]
        conv_sb = held.tile([P, KB, N], BF16, name="conv_sb")
        q_row = held.tile([1, D * N], F32, name="q_row")
        b_ru_rows = held.tile([D * 2, P], F32, name="b_ru_rows")
        b_c_rows = held.tile([D, P], F32, name="b_c_rows")
        w_c_sb = held.tile([P, D * P], BF16, name="w_c_sb")
        x_sb = held.tile([P, N], BF16, name="x_sb")
        h_sb = held.tile([P, N], F32, name="h_sb")
        store = held.tile([P, S], F32, name="store")

        w_ru_blocks = w_ru.rearrange("(p kb) e -> p kb e", kb=KB)
        nc.sync.dma_start(q_row[:], q.rearrange("d j -> (d j)").unsqueeze(0))
        nc.scalar.dma_start(conv_sb[:], conv.rearrange("(p kb) j -> p kb j", kb=KB))
        nc.scalar.dma_start(b_ru_rows[:], b_ru.rearrange("(c p) o -> c (p o)", p=P))
        nc.scalar.dma_start(b_c_rows[:], b_c.rearrange("(c p) o -> c (p o)", p=P))
        nc.sync.dma_start(w_ru_sb[0][:], w_ru_blocks[:, :, 0 : 2 * P])
        nc.sync.dma_start(w_ru_sb[1][:], w_ru_blocks[:, :, 2 * P : 4 * P])
        nc.sync.dma_start(w_c_sb[:], w_c)
        nc.sync.dma_start(x_sb[:], x)
        nc.sync.dma_start(h_sb[:], h)
        nc.sync.dma_start(store[:], base)
        nc.sync.dma_start(offsets[:], offs)

        zeros = held.tile([P, D * N], BF16, name="zeros")
        nc.vector.memset(zeros[:], 0.0)
        q_bank = psum.tile([P, D * N], F32, name="q_bank")
        for i in range(WARM_UP_PRODUCTS):
            nc.tensor.matmul(q_bank[:], zeros[:, 0:P], zeros[:], start=True, stop=True)

        ones_row = held.tile([1, P], F32, name="ones_row")
        nc.vector.memset(ones_row[:], 1.0)
        identity = held.tile([D * 2, D * 2], F32, name="identity")
        nc.vector.memset(identity[:], 0.0)
        for k in range(D * 2):
            nc.vector.memset(identity[0 : k + 1, k : k + 1], 1.0)
        for k in range(1, D * 2):
            nc.vector.memset(identity[0:k, k : k + 1], 0.0)

        nc.tensor.matmul(q_bank[:], ones_row[:], q_row[:], start=True, stop=True)
        q_sb = held.tile([P, D * N], F32, name="q_sb")
        nc.vector.tensor_copy(q_sb[:], q_bank[:])

        bias_bank = psum.tile([P, D * 3], F32, name="bias_bank")
        nc.tensor.matmul(bias_bank[:, 0 : D * 2], b_ru_rows[:], identity[:], start=True, stop=True)
        ru_biases = held.tile([P, D * 2], F32, name="ru_biases")
        nc.vector.tensor_copy(ru_biases[:], bias_bank[:, 0 : D * 2])

        scaled = {}
        for gate in ("r", "u", "c"):
            scaled[gate] = held.tile([P, D, N], F32, name="scaled_" + gate)

        def product_and_scaling(gate, d, pairs, bias):
            bank = psum.tile([P, N], F32, name="bank_%s%d" % (gate, d))
            for k, (weights, moving) in enumerate(pairs):
                nc.tensor.matmul(bank[:], weights, moving, start=(k == 0), stop=(k == len(pairs) - 1))
            nc.vector.scalar_tensor_tensor(
                scaled[gate][:, d, :], bank[:], bias, q_sb[:, d * N : (d + 1) * N], ALU.add, ALU.mult
            )

        def mixed(gate):
            pre = held.tile([P, N], F32, name="pre_" + gate)
            nc.vector.tensor_tensor(pre[:], scaled[gate][:, 0, :], scaled[gate][:, 1, :], ALU.add)
            return pre

        for d in range(D):
            for g, gate in enumerate(("r", "u")):
                product_and_scaling(
                    gate,
                    d,
                    [(w_ru_sb[d][:, kb, g * P : (g + 1) * P], conv_sb[:, kb, :]) for kb in range(KB)],
                    ru_biases[:, 2 * d + g : 2 * d + g + 1],
                )

        nc.tensor.matmul(bias_bank[:, D * 2 : D * 3], b_c_rows[:], identity[0:D, 0:D], start=True, stop=True)

        pre_r = mixed("r")
        r = held.tile([P, N], F32, name="r")
        nc.scalar.activation(r[:], pre_r[:], FUNC.Sigmoid)

        pre_u = mixed("u")
        one_minus_u = held.tile([P, N], F32, name="one_minus_u")
        nc.scalar.activation(one_minus_u[:], pre_u[:], FUNC.Sigmoid, scale=-1.0)
        u = held.tile([P, N], F32, name="u")
        nc.scalar.activation(u[:], pre_u[:], FUNC.Sigmoid)

        for d in range(D):
            product_and_scaling(
                "c", d, [(w_c_sb[:, d * P : (d + 1) * P], x_sb[:])], bias_bank[:, D * 2 + d : D * 2 + d + 1]
            )
        pre_c = mixed("c")
        cand = held.tile([P, N], F32, name="cand")
        nc.scalar.activation(cand[:], pre_c[:], FUNC.Tanh)

        r_h = held.tile([P, N], F32, name="r_h")
        nc.vector.tensor_tensor(r_h[:], r[:], h_sb[:], ALU.mult)
        kept = held.tile([P, N], F32, name="kept")
        nc.vector.tensor_tensor(kept[:], one_minus_u[:], r_h[:], ALU.mult)
        fresh = held.tile([P, N], F32, name="fresh")
        nc.vector.tensor_tensor(fresh[:], u[:], cand[:], ALU.mult)
        nc.vector.tensor_tensor(store[:].indirect(offsets[:]), kept[:], fresh[:], ALU.add)

        nc.sync.dma_start(out, store[:])
